import numpy as np
import ml_dtypes

BF16 = ml_dtypes.bfloat16


def bf(x):
    return np.asarray(x, np.float32).astype(BF16)


def f32(x):
    return np.asarray(x, np.float32)


def f64(x):
    return np.asarray(x).astype(np.float64)


def striped(idx):
    return np.tile(idx.reshape(-1, 16).T, (8, 1))


C, S, N = 256, 4096, 2048
P = 0.5


def setup_inputs():
    return {"base": f32(0.5 + np.random.random((C, S))), "sub": f32(0.5 + np.random.random((C, N))), "keep": f32(np.random.random((C, N)) >= P), "offs": striped(np.random.permutation(S)[:N])}


def reference(base, sub, keep, offs):
    idx = offs[:16].T.reshape(-1)
    s = f64(sub)
    z = s * f64(keep)
    comp = (s.sum(axis=1, keepdims=True) - z.sum(axis=1, keepdims=True)) / N
    res = f64(base).copy()
    res[:, idx] = z + comp
    return res

@@ -1,0 +1,53 @@
+import concourse.mybir as mybir
+
+F32 = mybir.dt.float32
+U16 = mybir.dt.uint16
+ALU = mybir.AluOpType
+COPY = mybir.ActivationFunctionType.Copy
+
+P = 128
+C = 256
+S = 4096
+N = 2048
+
+BYTES = 4 * (C * (S - N) + 2 * C * N + C * S) + 2 * N
+
+
+def tile_dropout_partial_binary_s_kernel(tc, base, sub, keep, offs, out):
+    nc = tc.nc
+    with (
+        tc.tile_pool(name="lists", bufs=1) as lists,
+        tc.tile_pool(name="rows", bufs=2) as rows,
+        tc.tile_pool(name="sums", bufs=2) as sums,
+    ):
+        offsets = lists.tile([P, N // 16], U16, name="offsets")
+        nc.sync.dma_start(offsets[:], offs)
+
+        for first_row in range(0, C, P):
+            block = slice(first_row, first_row + P)
+
+            sub_rows = rows.tile([P, N], F32)
+            nc.sync.dma_start(sub_rows[:], sub[block, :])
+            keep_rows = rows.tile([P, N], F32)
+            nc.sync.dma_start(keep_rows[:], keep[block, :])
+            window = rows.tile([P, S], F32)
+            nc.sync.dma_start(window[:], base[block, :])
+
+            unused_copy = rows.tile([P, N], F32)
+            sub_sum = sums.tile([P, 1], F32)
+            nc.scalar.activation(unused_copy[:], sub_rows[:], COPY, accum_out=sub_sum[:])
+
+            z = rows.tile([P, N], F32)
+            z_sum = sums.tile([P, 1], F32)
+            nc.vector.scalar_tensor_tensor(
+                z[:], sub_rows[:], 1.0, keep_rows[:], ALU.mult, ALU.mult, accum_out=z_sum[:]
+            )
+
+            comp = rows.tile([P, N], F32)
+            nc.vector.tensor_scalar(
+                comp[:], sub_sum[:].to_broadcast([P, N]), z_sum[:], 1.0 / N, ALU.subtract, ALU.mult
+            )
+
+            nc.vector.tensor_tensor(window[:].indirect(offsets[:]), z[:], comp[:], ALU.add)
+
+            nc.sync.dma_start(out[block, :], window[:])

@@ -17,6 +17,7 @@ def tile_dropout_partial_binary_s_kernel(tc, base, sub, keep, offs, out):
     nc = tc.nc
     with (
         tc.tile_pool(name="lists", bufs=1) as lists,
+        tc.tile_pool(name="windows", bufs=1) as windows,
         tc.tile_pool(name="rows", bufs=2) as rows,
         tc.tile_pool(name="sums", bufs=2) as sums,
     ):
@@ -30,7 +31,7 @@ def tile_dropout_partial_binary_s_kernel(tc, base, sub, keep, offs, out):
             nc.sync.dma_start(sub_rows[:], sub[block, :])
             keep_rows = rows.tile([P, N], F32)
             nc.sync.dma_start(keep_rows[:], keep[block, :])
-            window = rows.tile([P, S], F32)
+            window = windows.tile([P, S], F32, name=f"window_{first_row}")
             nc.sync.dma_start(window[:], base[block, :])
 
             unused_copy = rows.tile([P, N], F32)

@@ -9,6 +9,7 @@ P = 128
 C = 256
 S = 4096
 N = 2048
+BLOCKS = C // P
 
 BYTES = 4 * (C * (S - N) + 2 * C * N + C * S) + 2 * N
 
@@ -17,27 +18,29 @@ def tile_dropout_partial_binary_s_kernel(tc, base, sub, keep, offs, out):
     nc = tc.nc
     with (
         tc.tile_pool(name="lists", bufs=1) as lists,
-        tc.tile_pool(name="windows", bufs=1) as windows,
-        tc.tile_pool(name="rows", bufs=2) as rows,
-        tc.tile_pool(name="sums", bufs=2) as sums,
+        tc.tile_pool(name="rows", bufs=BLOCKS) as rows,
+        tc.tile_pool(name="sums", bufs=BLOCKS) as sums,
     ):
         offsets = lists.tile([P, N // 16], U16, name="offsets")
         nc.sync.dma_start(offsets[:], offs)
 
-        for first_row in range(0, C, P):
-            block = slice(first_row, first_row + P)
-
+        loaded = []
+        for b in range(BLOCKS):
+            block = slice(b * P, (b + 1) * P)
             sub_rows = rows.tile([P, N], F32)
             nc.sync.dma_start(sub_rows[:], sub[block, :])
             keep_rows = rows.tile([P, N], F32)
             nc.sync.dma_start(keep_rows[:], keep[block, :])
-            window = windows.tile([P, S], F32, name=f"window_{first_row}")
+            window = rows.tile([P, S], F32)
             nc.sync.dma_start(window[:], base[block, :])
 
             unused_copy = rows.tile([P, N], F32)
             sub_sum = sums.tile([P, 1], F32)
             nc.scalar.activation(unused_copy[:], sub_rows[:], COPY, accum_out=sub_sum[:])
 
+            loaded.append((block, sub_rows, keep_rows, window, sub_sum))
+
+        for block, sub_rows, keep_rows, window, sub_sum in loaded:
             z = rows.tile([P, N], F32)
             z_sum = sums.tile([P, 1], F32)
             nc.vector.scalar_tensor_tensor(

@@ -4,12 +4,15 @@ F32 = mybir.dt.float32
 U16 = mybir.dt.uint16
 ALU = mybir.AluOpType
 COPY = mybir.ActivationFunctionType.Copy
+IDENTITY = mybir.ActivationFunctionType.Identity
 
 P = 128
 C = 256
 S = 4096
 N = 2048
 BLOCKS = C // P
+
+VECTOR_COLUMNS = 3 * N // 4
 
 BYTES = 4 * (C * (S - N) + 2 * C * N + C * S) + 2 * N
 
@@ -36,7 +39,9 @@ def tile_dropout_partial_binary_s_kernel(tc, base, sub, keep, offs, out):
 
             unused_copy = rows.tile([P, N], F32)
             sub_sum = sums.tile([P, 1], F32)
-            nc.scalar.activation(unused_copy[:], sub_rows[:], COPY, accum_out=sub_sum[:])
+            nc.scalar.activation(
+                unused_copy[:], sub_rows[:], COPY, scale=1.0 / N, accum_out=sub_sum[:]
+            )
 
             loaded.append((block, sub_rows, keep_rows, window, sub_sum))
 
@@ -49,7 +54,19 @@ def tile_dropout_partial_binary_s_kernel(tc, base, sub, keep, offs, out):
 
             comp = rows.tile([P, N], F32)
             nc.vector.tensor_scalar(
-                comp[:], sub_sum[:].to_broadcast([P, N]), z_sum[:], 1.0 / N, ALU.subtract, ALU.mult
+                comp[:, :VECTOR_COLUMNS],
+                z_sum[:].to_broadcast([P, VECTOR_COLUMNS]),
+                -1.0 / N,
+                sub_sum[:],
+                ALU.mult,
+                ALU.add,
+            )
+            nc.scalar.activation(
+                comp[:, VECTOR_COLUMNS:],
+                z_sum[:].to_broadcast([P, N - VECTOR_COLUMNS]),
+                IDENTITY,
+                bias=sub_sum[:],
+                scale=-1.0 / N,
             )
 
             nc.vector.tensor_tensor(window[:].indirect(offsets[:]), z[:], comp[:], ALU.add)

@@ -1,18 +1,25 @@
 import concourse.mybir as mybir
+from concourse.masks import make_identity
 
 F32 = mybir.dt.float32
+BF16 = mybir.dt.bfloat16
 U16 = mybir.dt.uint16
 ALU = mybir.AluOpType
 COPY = mybir.ActivationFunctionType.Copy
 IDENTITY = mybir.ActivationFunctionType.Identity
+RELU = mybir.ActivationFunctionType.Relu
 
 P = 128
 C = 256
 S = 4096
 N = 2048
-BLOCKS = C // P
+BANK = 512
+CHUNKS = N // BANK
+HALF = N // 2
 
 VECTOR_COLUMNS = 3 * N // 4
+
+HUGE = 2.0**126
 
 BYTES = 4 * (C * (S - N) + 2 * C * N + C * S) + 2 * N
 
@@ -21,54 +28,128 @@ def tile_dropout_partial_binary_s_kernel(tc, base, sub, keep, offs, out):
     nc = tc.nc
     with (
         tc.tile_pool(name="lists", bufs=1) as lists,
-        tc.tile_pool(name="rows", bufs=BLOCKS) as rows,
-        tc.tile_pool(name="sums", bufs=BLOCKS) as sums,
+        tc.tile_pool(name="weights", bufs=1) as weights,
+        tc.tile_pool(name="rows", bufs=1) as rows,
+        tc.tile_pool(name="sums", bufs=1) as sums,
+        tc.psum_pool(name="psum", bufs=1) as psum,
     ):
         offsets = lists.tile([P, N // 16], U16, name="offsets")
         nc.sync.dma_start(offsets[:], offs)
 
-        loaded = []
-        for b in range(BLOCKS):
-            block = slice(b * P, (b + 1) * P)
-            sub_rows = rows.tile([P, N], F32)
-            nc.sync.dma_start(sub_rows[:], sub[block, :])
-            keep_rows = rows.tile([P, N], F32)
-            nc.sync.dma_start(keep_rows[:], keep[block, :])
-            window = rows.tile([P, S], F32)
-            nc.sync.dma_start(window[:], base[block, :])
+        first, second = slice(0, P), slice(P, 2 * P)
+        sub0 = rows.tile([P, N], F32)
+        nc.sync.dma_start(sub0[:], sub[first, :])
+        keep0 = rows.tile([P, N], F32)
+        nc.sync.dma_start(keep0[:], keep[first, :])
+        window0 = rows.tile([P, S], F32)
+        nc.sync.dma_start(window0[:], base[first, :])
+        keep1 = rows.tile([P, N], F32)
+        sub1 = rows.tile([P, N], F32)
+        for half in (slice(0, HALF), slice(HALF, N)):
+            nc.sync.dma_start(keep1[:, half], keep[second, half])
+            nc.sync.dma_start(sub1[:, half], sub[second, half])
+        window1 = rows.tile([P, S], F32)
+        nc.sync.dma_start(window1[:], base[second, :])
 
-            unused_copy = rows.tile([P, N], F32)
-            sub_sum = sums.tile([P, 1], F32)
+        identity = weights.tile([P, P], F32)
+        make_identity(nc, identity[:])
+        plus_huge = weights.tile([P, P], BF16)
+        nc.scalar.activation(plus_huge[:], identity[:], COPY, scale=HUGE)
+        minus_huge = weights.tile([P, P], BF16)
+        nc.scalar.activation(minus_huge[:], identity[:], COPY, scale=-HUGE)
+        ones = weights.tile([P, BANK], BF16)
+        nc.gpsimd.memset(ones[:], 1.0)
+
+        unused_copy = rows.tile([P, N], F32)
+        sub0_sum = sums.tile([P, 1], F32)
+        nc.scalar.activation(
+            unused_copy[:], sub0[:], COPY, scale=1.0 / N, accum_out=sub0_sum[:]
+        )
+        z0 = rows.tile([P, N], F32)
+        z0_sum = sums.tile([P, 1], F32)
+        nc.vector.scalar_tensor_tensor(
+            z0[:], sub0[:], 1.0, keep0[:], ALU.mult, ALU.mult, accum_out=z0_sum[:]
+        )
+        comp0 = rows.tile([P, N], F32)
+        nc.vector.tensor_scalar(
+            comp0[:, :VECTOR_COLUMNS],
+            z0_sum[:].to_broadcast([P, VECTOR_COLUMNS]),
+            -1.0 / N,
+            sub0_sum[:],
+            ALU.mult,
+            ALU.add,
+        )
+        nc.scalar.activation(
+            comp0[:, VECTOR_COLUMNS:],
+            z0_sum[:].to_broadcast([P, N - VECTOR_COLUMNS]),
+            IDENTITY,
+            bias=sub0_sum[:],
+            scale=-1.0 / N,
+        )
+        nc.vector.tensor_tensor(window0[:].indirect(offsets[:]), z0[:], comp0[:], ALU.add)
+        nc.sync.dma_start(out[first, :], window0[:])
+
+        keep_halves = keep1[:].bitcast(BF16)
+        low = []
+        high = []
+        for k in range(CHUNKS):
+            low_bank = psum.tile([P, BANK], F32, name=f"low{k}")
+            nc.tensor.matmul(low_bank[:], minus_huge[:], ones[:], start=True, stop=False)
+            low.append(low_bank)
+            high_bank = psum.tile([P, BANK], F32, name=f"high{k}")
+            nc.tensor.matmul(high_bank[:], plus_huge[:], ones[:], start=True, stop=False)
+            high.append(high_bank)
+
+        minuends = sums.tile([P, 2 + CHUNKS], F32)
+        subtrahends = sums.tile([P, CHUNKS + 1], F32)
+        positive = rows.tile([P, N], F32)
+        negative = rows.tile([P, N], F32)
+        for h in range(2):
+            half = slice(h * HALF, (h + 1) * HALF)
+            in_half = range(h * CHUNKS // 2, (h + 1) * CHUNKS // 2)
+            for k in in_half:
+                kept = keep_halves[:, 2 * k * BANK + 1 : 2 * (k + 1) * BANK : 2]
+                nc.tensor.matmul(low[k][:], plus_huge[:], kept, start=False, stop=False)
+                nc.tensor.matmul(high[k][:], minus_huge[:], kept, start=False, stop=False)
             nc.scalar.activation(
-                unused_copy[:], sub_rows[:], COPY, scale=1.0 / N, accum_out=sub_sum[:]
+                unused_copy[:, half], sub1[:, half], COPY, accum_out=minuends[:, h : h + 1]
             )
-
-            loaded.append((block, sub_rows, keep_rows, window, sub_sum))
-
-        for block, sub_rows, keep_rows, window, sub_sum in loaded:
-            z = rows.tile([P, N], F32)
-            z_sum = sums.tile([P, 1], F32)
-            nc.vector.scalar_tensor_tensor(
-                z[:], sub_rows[:], 1.0, keep_rows[:], ALU.mult, ALU.mult, accum_out=z_sum[:]
-            )
-
-            comp = rows.tile([P, N], F32)
-            nc.vector.tensor_scalar(
-                comp[:, :VECTOR_COLUMNS],
-                z_sum[:].to_broadcast([P, VECTOR_COLUMNS]),
-                -1.0 / N,
-                sub_sum[:],
-                ALU.mult,
-                ALU.add,
-            )
-            nc.scalar.activation(
-                comp[:, VECTOR_COLUMNS:],
-                z_sum[:].to_broadcast([P, N - VECTOR_COLUMNS]),
-                IDENTITY,
-                bias=sub_sum[:],
-                scale=-1.0 / N,
-            )
-
-            nc.vector.tensor_tensor(window[:].indirect(offsets[:]), z[:], comp[:], ALU.add)
-
-            nc.sync.dma_start(out[block, :], window[:])
+            for k in in_half:
+                columns = slice(k * BANK, (k + 1) * BANK)
+                nc.tensor.matmul(
+                    low[k][:], identity[:], sub1[:, columns], start=False, stop=True
+                )
+                nc.scalar.activation(
+                    positive[:, columns], low[k][:], RELU,
+                    accum_out=subtrahends[:, k : k + 1],
+                )
+                nc.tensor.matmul(
+                    high[k][:], identity[:], sub1[:, columns], start=False, stop=True
+                )
+                nc.scalar.activation(
+                    negative[:, columns], high[k][:], RELU, scale=-1.0,
+                    accum_out=minuends[:, 2 + k : 3 + k],
+                )
+        unused_minuends = sums.tile([P, 2 + CHUNKS], F32)
+        nc.scalar.activation(
+            unused_minuends[:], minuends[:], COPY, scale=-1.0,
+            accum_out=subtrahends[:, CHUNKS : CHUNKS + 1],
+        )
+        unused_subtrahends = sums.tile([P, CHUNKS + 1], F32)
+        comp1 = sums.tile([P, 1], F32)
+        nc.scalar.activation(
+            unused_subtrahends[:], subtrahends[:], COPY, scale=-1.0 / N, accum_out=comp1[:]
+        )
+        lowered_comp = rows.tile([P, N], F32)
+        nc.vector.tensor_scalar(
+            lowered_comp[:, :VECTOR_COLUMNS], negative[:, :VECTOR_COLUMNS],
+            -1.0, comp1[:], ALU.mult, ALU.add,
+        )
+        nc.scalar.activation(
+            lowered_comp[:, VECTOR_COLUMNS:], negative[:, VECTOR_COLUMNS:],
+            IDENTITY, bias=comp1[:], scale=-1.0,
+        )
+        nc.vector.tensor_tensor(
+            window1[:].indirect(offsets[:]), positive[:], lowered_comp[:], ALU.add
+        )
+        nc.sync.dma_start(out[second, :], window1[:])

@@ -45,9 +45,10 @@ def tile_dropout_partial_binary_s_kernel(tc, base, sub, keep, offs, out):
         nc.sync.dma_start(window0[:], base[first, :])
         keep1 = rows.tile([P, N], F32)
         sub1 = rows.tile([P, N], F32)
-        for half in (slice(0, HALF), slice(HALF, N)):
-            nc.sync.dma_start(keep1[:, half], keep[second, half])
-            nc.sync.dma_start(sub1[:, half], sub[second, half])
+        chunks = [slice(k * BANK, (k + 1) * BANK) for k in range(CHUNKS)]
+        for columns in chunks:
+            nc.sync.dma_start(keep1[:, columns], keep[second, columns])
+            nc.sync.dma_start(sub1[:, columns], sub[second, columns])
         window1 = rows.tile([P, S], F32)
         nc.sync.dma_start(window1[:], base[second, :])
 
@@ -100,41 +101,33 @@ def tile_dropout_partial_binary_s_kernel(tc, base, sub, keep, offs, out):
             nc.tensor.matmul(high_bank[:], plus_huge[:], ones[:], start=True, stop=False)
             high.append(high_bank)
 
-        minuends = sums.tile([P, 2 + CHUNKS], F32)
+        minuends = sums.tile([P, 2 * CHUNKS], F32)
         subtrahends = sums.tile([P, CHUNKS + 1], F32)
         positive = rows.tile([P, N], F32)
         negative = rows.tile([P, N], F32)
-        for h in range(2):
-            half = slice(h * HALF, (h + 1) * HALF)
-            in_half = range(h * CHUNKS // 2, (h + 1) * CHUNKS // 2)
-            for k in in_half:
-                kept = keep_halves[:, 2 * k * BANK + 1 : 2 * (k + 1) * BANK : 2]
-                nc.tensor.matmul(low[k][:], plus_huge[:], kept, start=False, stop=False)
-                nc.tensor.matmul(high[k][:], minus_huge[:], kept, start=False, stop=False)
+        for k, columns in enumerate(chunks):
+            kept = keep_halves[:, 2 * k * BANK + 1 : 2 * (k + 1) * BANK : 2]
+            nc.tensor.matmul(low[k][:], plus_huge[:], kept, start=False, stop=False)
+            nc.tensor.matmul(high[k][:], minus_huge[:], kept, start=False, stop=False)
+            nc.tensor.matmul(high[k][:], identity[:], sub1[:, columns], start=False, stop=True)
+            nc.tensor.matmul(low[k][:], identity[:], sub1[:, columns], start=False, stop=True)
             nc.scalar.activation(
-                unused_copy[:, half], sub1[:, half], COPY, accum_out=minuends[:, h : h + 1]
+                unused_copy[:, columns], sub1[:, columns], COPY,
+                accum_out=minuends[:, k : k + 1],
             )
-            for k in in_half:
-                columns = slice(k * BANK, (k + 1) * BANK)
-                nc.tensor.matmul(
-                    low[k][:], identity[:], sub1[:, columns], start=False, stop=True
-                )
+            nc.scalar.activation(
+                negative[:, columns], high[k][:], RELU, scale=-1.0,
+                accum_out=minuends[:, CHUNKS + k : CHUNKS + k + 1],
+            )
+            if k == CHUNKS - 1:
+                unused_minuends = sums.tile([P, 2 * CHUNKS], F32)
                 nc.scalar.activation(
-                    positive[:, columns], low[k][:], RELU,
-                    accum_out=subtrahends[:, k : k + 1],
+                    unused_minuends[:], minuends[:], COPY, scale=-1.0,
+                    accum_out=subtrahends[:, CHUNKS : CHUNKS + 1],
                 )
-                nc.tensor.matmul(
-                    high[k][:], identity[:], sub1[:, columns], start=False, stop=True
-                )
-                nc.scalar.activation(
-                    negative[:, columns], high[k][:], RELU, scale=-1.0,
-                    accum_out=minuends[:, 2 + k : 3 + k],
-                )
-        unused_minuends = sums.tile([P, 2 + CHUNKS], F32)
-        nc.scalar.activation(
-            unused_minuends[:], minuends[:], COPY, scale=-1.0,
-            accum_out=subtrahends[:, CHUNKS : CHUNKS + 1],
-        )
+            nc.scalar.activation(
+                positive[:, columns], low[k][:], RELU, accum_out=subtrahends[:, k : k + 1]
+            )
         unused_subtrahends = sums.tile([P, CHUNKS + 1], F32)
         comp1 = sums.tile([P, 1], F32)
         nc.scalar.activation(
@@ -142,11 +135,11 @@ def tile_dropout_partial_binary_s_kernel(tc, base, sub, keep, offs, out):
         )
         lowered_comp = rows.tile([P, N], F32)
         nc.vector.tensor_scalar(
-            lowered_comp[:, :VECTOR_COLUMNS], negative[:, :VECTOR_COLUMNS],
+            lowered_comp[:, :HALF], negative[:, :HALF],
             -1.0, comp1[:], ALU.mult, ALU.add,
         )
         nc.scalar.activation(
-            lowered_comp[:, VECTOR_COLUMNS:], negative[:, VECTOR_COLUMNS:],
+            lowered_comp[:, HALF:], negative[:, HALF:],
             IDENTITY, bias=comp1[:], scale=-1.0,
         )
         nc.vector.tensor_tensor(

import concourse.mybir as mybir
from concourse.masks import make_identity

F32 = mybir.dt.float32
BF16 = mybir.dt.bfloat16
U16 = mybir.dt.uint16
ALU = mybir.AluOpType
COPY = mybir.ActivationFunctionType.Copy
IDENTITY = mybir.ActivationFunctionType.Identity
RELU = mybir.ActivationFunctionType.Relu

P = 128
C = 256
S = 4096
N = 2048
BANK = 512
CHUNKS = N // BANK
HALF = N // 2

VECTOR_COLUMNS = 3 * N // 4

HUGE = 2.0**126

BYTES = 4 * (C * (S - N) + 2 * C * N + C * S) + 2 * N


def tile_dropout_partial_binary_s_kernel(tc, base, sub, keep, offs, out):
    nc = tc.nc
    with (
        tc.tile_pool(name="lists", bufs=1) as lists,
        tc.tile_pool(name="weights", bufs=1) as weights,
        tc.tile_pool(name="rows", bufs=1) as rows,
        tc.tile_pool(name="sums", bufs=1) as sums,
        tc.psum_pool(name="psum", bufs=1) as psum,
    ):
        offsets = lists.tile([P, N // 16], U16, name="offsets")
        nc.sync.dma_start(offsets[:], offs)

        first, second = slice(0, P), slice(P, 2 * P)
        sub0 = rows.tile([P, N], F32)
        nc.sync.dma_start(sub0[:], sub[first, :])
        keep0 = rows.tile([P, N], F32)
        nc.sync.dma_start(keep0[:], keep[first, :])
        window0 = rows.tile([P, S], F32)
        nc.sync.dma_start(window0[:], base[first, :])
        keep1 = rows.tile([P, N], F32)
        sub1 = rows.tile([P, N], F32)
        chunks = [slice(k * BANK, (k + 1) * BANK) for k in range(CHUNKS)]
        for columns in chunks:
            nc.sync.dma_start(keep1[:, columns], keep[second, columns])
            nc.sync.dma_start(sub1[:, columns], sub[second, columns])
        window1 = rows.tile([P, S], F32)
        nc.sync.dma_start(window1[:], base[second, :])

        identity = weights.tile([P, P], F32)
        make_identity(nc, identity[:])
        plus_huge = weights.tile([P, P], BF16)
        nc.scalar.activation(plus_huge[:], identity[:], COPY, scale=HUGE)
        minus_huge = weights.tile([P, P], BF16)
        nc.scalar.activation(minus_huge[:], identity[:], COPY, scale=-HUGE)
        ones = weights.tile([P, BANK], BF16)
        nc.gpsimd.memset(ones[:], 1.0)

        unused_copy = rows.tile([P, N], F32)
        sub0_sum = sums.tile([P, 1], F32)
        nc.scalar.activation(
            unused_copy[:], sub0[:], COPY, scale=1.0 / N, accum_out=sub0_sum[:]
        )
        z0 = rows.tile([P, N], F32)
        z0_sum = sums.tile([P, 1], F32)
        nc.vector.scalar_tensor_tensor(
            z0[:], sub0[:], 1.0, keep0[:], ALU.mult, ALU.mult, accum_out=z0_sum[:]
        )
        comp0 = rows.tile([P, N], F32)
        nc.vector.tensor_scalar(
            comp0[:, :VECTOR_COLUMNS],
            z0_sum[:].to_broadcast([P, VECTOR_COLUMNS]),
            -1.0 / N,
            sub0_sum[:],
            ALU.mult,
            ALU.add,
        )
        nc.scalar.activation(
            comp0[:, VECTOR_COLUMNS:],
            z0_sum[:].to_broadcast([P, N - VECTOR_COLUMNS]),
            IDENTITY,
            bias=sub0_sum[:],
            scale=-1.0 / N,
        )
        nc.vector.tensor_tensor(window0[:].indirect(offsets[:]), z0[:], comp0[:], ALU.add)
        nc.sync.dma_start(out[first, :], window0[:])

        keep_halves = keep1[:].bitcast(BF16)
        low = []
        high = []
        for k in range(CHUNKS):
            low_bank = psum.tile([P, BANK], F32, name=f"low{k}")
            nc.tensor.matmul(low_bank[:], minus_huge[:], ones[:], start=True, stop=False)
            low.append(low_bank)
            high_bank = psum.tile([P, BANK], F32, name=f"high{k}")
            nc.tensor.matmul(high_bank[:], plus_huge[:], ones[:], start=True, stop=False)
            high.append(high_bank)

        minuends = sums.tile([P, 2 * CHUNKS], F32)
        subtrahends = sums.tile([P, CHUNKS + 1], F32)
        positive = rows.tile([P, N], F32)
        negative = rows.tile([P, N], F32)
        for k, columns in enumerate(chunks):
            kept = keep_halves[:, 2 * k * BANK + 1 : 2 * (k + 1) * BANK : 2]
            nc.tensor.matmul(low[k][:], plus_huge[:], kept, start=False, stop=False)
            nc.tensor.matmul(high[k][:], minus_huge[:], kept, start=False, stop=False)
            nc.tensor.matmul(high[k][:], identity[:], sub1[:, columns], start=False, stop=True)
            nc.tensor.matmul(low[k][:], identity[:], sub1[:, columns], start=False, stop=True)
            nc.scalar.activation(
                unused_copy[:, columns], sub1[:, columns], COPY,
                accum_out=minuends[:, k : k + 1],
            )
            nc.scalar.activation(
                negative[:, columns], high[k][:], RELU, scale=-1.0,
                accum_out=minuends[:, CHUNKS + k : CHUNKS + k + 1],
            )
            if k == CHUNKS - 1:
                unused_minuends = sums.tile([P, 2 * CHUNKS], F32)
                nc.scalar.activation(
                    unused_minuends[:], minuends[:], COPY, scale=-1.0,
                    accum_out=subtrahends[:, CHUNKS : CHUNKS + 1],
                )
            nc.scalar.activation(
                positive[:, columns], low[k][:], RELU, accum_out=subtrahends[:, k : k + 1]
            )
        unused_subtrahends = sums.tile([P, CHUNKS + 1], F32)
        comp1 = sums.tile([P, 1], F32)
        nc.scalar.activation(
            unused_subtrahends[:], subtrahends[:], COPY, scale=-1.0 / N, accum_out=comp1[:]
        )
        lowered_comp = rows.tile([P, N], F32)
        nc.vector.tensor_scalar(
            lowered_comp[:, :HALF], negative[:, :HALF],
            -1.0, comp1[:], ALU.mult, ALU.add,
        )
        nc.scalar.activation(
            lowered_comp[:, HALF:], negative[:, HALF:],
            IDENTITY, bias=comp1[:], scale=-1.0,
        )
        nc.vector.tensor_tensor(
            window1[:].indirect(offsets[:]), positive[:], lowered_comp[:], ALU.add
        )
        nc.sync.dma_start(out[second, :], window1[:])
